import numpy as np
import ml_dtypes


BF16 = ml_dtypes.bfloat16


def bf(x):
    return np.asarray(x, np.float32).astype(BF16)


def f64(x):
    return np.asarray(x).astype(np.float64)


E2M1 = np.array([0.0, 0.5, 1.0, 1.5, 2.0, 3.0, 4.0, 6.0, -0.0, -0.5, -1.0, -1.5, -2.0, -3.0, -4.0, -6.0])


def pack_weight(w, fmt):
    k, n = w.shape
    w = f64(bf(w)).reshape(k // 32, 32, n)
    amax = np.abs(w).max(1)
    if fmt == "e4m3":
        byte = np.frexp(amax)[1] - 1 + 127 - 7
    else:
        mant, ex = np.frexp(amax / 6.0)
        byte = np.where(mant > 0.5, ex, ex - 1) + 127
    byte = np.clip(np.where(amax > 0, byte, 1), 1, 254)
    scaled = (w * np.exp2(127.0 - byte)[:, None, :]).reshape(k, n).astype(np.float32)
    by_word = np.ascontiguousarray(scaled.reshape(k // 512, 128, 4, n).transpose(0, 1, 3, 2))
    if fmt == "e4m3":
        words = by_word.astype(ml_dtypes.float8_e4m3fn).view(np.uint8)
    else:
        c = by_word.astype(ml_dtypes.float4_e2m1fn).view(np.uint8) & 0xF
        words = c[..., 0::2] | (c[..., 1::2] << 4)
    return np.ascontiguousarray(words), np.ascontiguousarray(byte.astype(np.uint8).reshape(k // 512, 16, n))


def unpack_weight(words, scales, fmt):
    g, p, n, _ = words.shape
    if fmt == "e4m3":
        vals = np.ascontiguousarray(words).view(ml_dtypes.float8_e4m3fn).astype(np.float64)
    else:
        nib = np.empty((g, p, n, 4), np.uint8)
        nib[..., 0::2] = words & 0xF
        nib[..., 1::2] = words >> 4
        vals = E2M1[nib]
    vals = vals * np.repeat(np.exp2(scales.astype(np.float64) - 127.0), 8, axis=1)[..., None]
    return vals.transpose(0, 1, 3, 2).reshape(g * 512, n)

def pack4(w):
    words, scales = pack_weight(w, "e2m1")
    return words.reshape(words.shape[0], 128, -1), scales


def unpack4(words, scales):
    return unpack_weight(words.reshape(words.shape[0], 128, -1, 2), scales, "e2m1")


def kspread(k):
    return np.exp2(np.repeat(np.random.randint(-6, 7, k // 32), 32).astype(np.float64))


B, H, L, G, P = 128, 2048, 4, 4, 2


def sigmoid(v):
    return 1.0 / (1.0 + np.exp(-v))


def setup_inputs():
    s, t = kspread(H), kspread(H)
    sc = 1.0 / np.sqrt(H)
    lstm_input = np.random.standard_normal((B, H)) * 0.5 * s
    h_prev = np.random.standard_normal((B, H)) * t
    c_prev = bf(np.random.standard_normal((B, H)))
    w_ih = np.random.standard_normal((G * H, H)) * sc / s[None, :]
    w_hh = np.random.standard_normal((G * H, H)) * sc / t[None, :]
    b_ih = bf(np.random.standard_normal(G * H) * 0.3)
    b_hh = bf(np.random.standard_normal(G * H) * 0.3)
    lstm_input_words, lstm_input_scales = pack4(np.ascontiguousarray(lstm_input.T))
    h_prev_words, h_prev_scales = pack4(np.ascontiguousarray(h_prev.T))
    w_ih_words, w_ih_scales = pack4(np.ascontiguousarray(w_ih.T))
    w_hh_words, w_hh_scales = pack4(np.ascontiguousarray(w_hh.T))
    return {"lstm_input_words": lstm_input_words,
            "lstm_input_scales": lstm_input_scales,
            "h_prev_words": h_prev_words,
            "h_prev_scales": h_prev_scales,
            "c_prev": c_prev,
            "w_ih_words": w_ih_words,
            "w_ih_scales": w_ih_scales,
            "w_hh_words": w_hh_words,
            "w_hh_scales": w_hh_scales,
            "b_ih": b_ih,
            "b_hh": b_hh}


def reference(lstm_input_words, lstm_input_scales, h_prev_words, h_prev_scales, c_prev, w_ih_words, w_ih_scales, w_hh_words, w_hh_scales, b_ih, b_hh):
    gates = ((unpack4(lstm_input_words, lstm_input_scales).T @ unpack4(w_ih_words, w_ih_scales)) + f64(b_ih)
             + (unpack4(h_prev_words, h_prev_scales).T @ unpack4(w_hh_words, w_hh_scales)) + f64(b_hh))
    i, f, g, o = np.split(gates, G, axis=-1)
    i = sigmoid(i)
    f = sigmoid(f)
    g = np.tanh(g)
    o = sigmoid(o)
    c_next = f * f64(c_prev) + i * g
    h_next = o * np.tanh(c_next)
    return h_next, c_next

@@ -1,0 +1,257 @@
+from contextlib import ExitStack
+
+import concourse.masks as masks
+import concourse.mybir as mybir
+
+FLOPS = 2 * 128 * 4096 * 8192
+
+F32 = mybir.dt.float32
+BF16 = mybir.dt.bfloat16
+U8 = mybir.dt.uint8
+I32 = mybir.dt.int32
+FP4X4 = mybir.dt.float4_e2m1fn_x4
+FUNC = mybir.ActivationFunctionType
+ALU = mybir.AluOpType
+
+P = 128
+H = 2048
+NT = 512
+TILES = H // NT
+GROUPS = 4
+GATE_BYTES = 2 * H
+TILE_BYTES = 2 * NT
+PAIR = 2 * H
+
+
+def load_scale_row_set(nc, plane, scales, r):
+    nc.sync.dma_start(
+        out=plane[r:P:32, :, :].bitcast(I32),
+        in_=scales[:, r:16:4, :].rearrange("g q n -> q g n").bitcast(I32),
+    )
+
+
+def load_codes(nc, pool, words, g0, ng, c0, nbytes):
+    codes = pool.tile([P, ng, nbytes], U8, name="codes", tag="codes", align_bytes=64)
+    nc.sync.dma_start(
+        out=codes[:].bitcast(I32),
+        in_=words[g0 : g0 + ng, :, c0 : c0 + nbytes].rearrange("g p n -> p g n").bitcast(I32),
+    )
+    return codes
+
+
+def tile_multilayerlstmcell_pa_kernel(
+    tc,
+    lstm_input_words,
+    lstm_input_scales,
+    h_prev_words,
+    h_prev_scales,
+    c_prev,
+    w_ih_words,
+    w_ih_scales,
+    w_hh_words,
+    w_hh_scales,
+    b_ih,
+    b_hh,
+    out_0,
+    out_1,
+):
+    nc = tc.nc
+    w_words = (w_ih_words, w_hh_words)
+    w_scales = (w_ih_scales, w_hh_scales)
+
+    with ExitStack() as ctx:
+        ctx.enter_context(tc.manual_schedule())
+        const = ctx.enter_context(tc.tile_pool(name="const", bufs=1))
+        stream = ctx.enter_context(tc.tile_pool(name="stream", bufs=8))
+        work = ctx.enter_context(tc.tile_pool(name="work", bufs=4))
+        psum = ctx.enter_context(tc.psum_pool(name="psum", bufs=8))
+
+        brow = const.tile([P, NT], BF16, name="brow")
+        nc.gpsimd.memset(brow[:], 0.0)
+        ident = const.tile([P, P], BF16, name="ident")
+        masks.make_identity(nc, ident[:])
+        warm = const.tile([P, 1], F32, name="warm")
+        nc.vector.memset(warm[:], 0.0)
+
+        nc.scalar.dma_start(out=brow[0:16, :], in_=b_ih.rearrange("(c n) -> c n", c=16))
+        nc.scalar.dma_start(out=brow[16:32, :], in_=b_hh.rearrange("(c n) -> c n", c=16))
+        cprev = const.tile([P, H], BF16, name="cprev")
+        nc.scalar.dma_start(out=cprev[:], in_=c_prev)
+        nc.scalar.activation(out=warm[:], in_=warm[:], func=FUNC.Sigmoid)
+
+        a_codes = []
+        a_plane = []
+        for m, (words, label) in enumerate(((lstm_input_words, "x"), (h_prev_words, "h"))):
+            codes = const.tile([P, GROUPS, 2 * P], U8, name="acodes_" + label, align_bytes=64)
+            plane = const.tile([P, GROUPS, P], U8, name="aplane_" + label, align_bytes=64)
+            nc.vector.memset(plane[:].rearrange("p g n -> p (g n)").bitcast(I32), 0)
+            nc.sync.dma_start(
+                out=codes[:].bitcast(I32), in_=words.rearrange("g p n -> p g n").bitcast(I32)
+            )
+            a_codes.append(codes)
+            a_plane.append(plane)
+
+        planes = [[None, None], [None, None]]
+        sel = const.tile([P, 16], BF16, name="sel")
+        for pair in range(2):
+            for m in range(2):
+                plane = const.tile(
+                    [P, GROUPS, PAIR], U8, name="plane_%d_%d" % (m, pair), align_bytes=64
+                )
+                nc.vector.memset(plane[:].rearrange("p g n -> p (g n)").bitcast(I32), 0)
+                planes[m][pair] = plane
+                if pair == 0 and m == 0:
+                    nc.vector.tensor_tensor(
+                        out=sel[:], in0=ident[:, 0:16], in1=ident[:, 16:32], op=ALU.add
+                    )
+
+        def load_gate_codes(gate):
+            return [
+                load_codes(nc, stream, w_words[m], 2 * half, 2, gate * GATE_BYTES, GATE_BYTES)
+                for m in range(2)
+                for half in range(2)
+            ]
+
+        def load_pair_scales(pair):
+            for m in range(2):
+                for r in range(4):
+                    load_scale_row_set(
+                        nc, planes[m][pair], w_scales[m][:, :, pair * PAIR : (pair + 1) * PAIR], r
+                    )
+
+        def mx_pass(acc, m, g, codes_ap, gate, t, start, stop):
+            col = (gate % 2) * H + t * NT
+            nc.tensor.matmul_mx(
+                out=acc[:],
+                lhsT=a_codes[m][:, g, :].bitcast(FP4X4),
+                lhsT_scale=a_plane[m][:, g, :],
+                rhs=codes_ap.bitcast(FP4X4),
+                rhs_scale=planes[m][gate // 2][:, g, col : col + NT],
+                start=start,
+                stop=stop,
+            )
+
+        def new_accs():
+            return [psum.tile([P, NT], F32, name="acc", tag="acc") for t in range(TILES)]
+
+        def gate_matmuls(gate, chunks, accs, ms):
+            for m in ms:
+                for half in range(2):
+                    chunk = chunks[2 * m + half]
+                    for j in range(2):
+                        g = 2 * half + j
+                        for t in range(TILES):
+                            mx_pass(
+                                accs[t],
+                                m,
+                                g,
+                                chunk[:, j, t * TILE_BYTES : (t + 1) * TILE_BYTES],
+                                gate,
+                                t,
+                                m == 0 and g == 0,
+                                m == 1 and g == GROUPS - 1,
+                            )
+
+        def add_bias(dst, acc, gate, t):
+            nc.vector.tensor_tensor(
+                out=dst[:], in0=acc[:], in1=bias[:, gate * TILES + t, :], op=ALU.add
+            )
+
+        small = [(a_plane[m], sc, r) for m, sc in enumerate((lstm_input_scales, h_prev_scales)) for r in range(4)]
+        chunks_i = []
+        for n in range(4):
+            chunks_i.append(load_codes(nc, stream, w_words[n // 2], 2 * (n % 2), 2, 0, GATE_BYTES))
+            for plane, sc, r in small[2 * n : 2 * n + 2]:
+                load_scale_row_set(nc, plane, sc, r)
+        load_pair_scales(0)
+
+        bias = const.tile([P, 4 * TILES, NT], F32, name="bias")
+        for c in range(4 * TILES):
+            bacc = psum.tile([P, NT], F32, name="acc", tag="acc")
+            nc.tensor.matmul(
+                out=bacc[:],
+                lhsT=sel[:, c : c + 1].to_broadcast([P, P]),
+                rhs=brow[:],
+                start=True,
+                stop=True,
+            )
+            nc.scalar.copy(out=bias[:, c, :], in_=bacc[:])
+
+        chunks_f = load_gate_codes(1)
+
+        accs = new_accs()
+        gate_matmuls(0, chunks_i, accs, (0, 1))
+        si = [const.tile([P, NT], F32, name="si%d" % t) for t in range(TILES)]
+        for t in range(TILES):
+            add_bias(si[t], accs[t], 0, t)
+        for t in range(TILES):
+            nc.scalar.activation(out=si[t][:], in_=si[t][:], func=FUNC.Sigmoid)
+
+        load_pair_scales(1)
+        chunks_g = load_gate_codes(2)
+
+        accs = new_accs()
+        gate_matmuls(1, chunks_f, accs, (0, 1))
+        fc = [const.tile([P, NT], F32, name="fc%d" % t) for t in range(TILES)]
+        for t in range(TILES):
+            add_bias(fc[t], accs[t], 1, t)
+        for t in range(TILES):
+            nc.scalar.activation(out=fc[t][:], in_=fc[t][:], func=FUNC.Sigmoid)
+        for t in range(TILES):
+            nc.vector.tensor_tensor(
+                out=fc[t][:], in0=fc[t][:], in1=cprev[:, t * NT : (t + 1) * NT], op=ALU.mult
+            )
+
+        o_col = 3 * GATE_BYTES
+        chunks_o = [load_codes(nc, stream, w_ih_words, 2 * half, 2, o_col, GATE_BYTES) for half in range(2)]
+        o_hh = [
+            [(load_codes(nc, stream, w_hh_words, 0, GROUPS, o_col + t * TILE_BYTES, TILE_BYTES), 0, GROUPS)]
+            for t in range(2)
+        ]
+
+        accs = new_accs()
+        gate_matmuls(2, chunks_g, accs, (0, 1))
+        cand = [work.tile([P, NT], F32, name="gate", tag="gate") for t in range(TILES)]
+        for t in range(TILES):
+            add_bias(cand[t], accs[t], 2, t)
+        for t in range(TILES):
+            nc.scalar.activation(out=cand[t][:], in_=cand[t][:], func=FUNC.Tanh)
+        for t in range(TILES):
+            nc.vector.tensor_tensor(out=cand[t][:], in0=cand[t][:], in1=si[t][:], op=ALU.mult)
+            nc.vector.tensor_tensor(out=fc[t][:], in0=cand[t][:], in1=fc[t][:], op=ALU.add)
+            nc.gpsimd.dma_start(out=out_1[:, t * NT : (t + 1) * NT], in_=fc[t][:])
+            nc.scalar.activation(out=si[t][:], in_=fc[t][:], func=FUNC.Tanh)
+
+        o_hh.append(
+            [(load_codes(nc, stream, w_hh_words, 0, GROUPS, o_col + 2 * TILE_BYTES, TILE_BYTES), 0, GROUPS)]
+        )
+        o_hh.append(
+            [
+                (load_codes(nc, stream, w_hh_words, 2 * half, 2, o_col + 3 * TILE_BYTES, TILE_BYTES), 2 * half, 2)
+                for half in range(2)
+            ]
+        )
+
+        accs = new_accs()
+        gate_matmuls(3, chunks_o, accs, (0,))
+        ogs = []
+
+        def o_front(t):
+            for codes, g0, ng in o_hh[t]:
+                for j in range(ng):
+                    mx_pass(accs[t], 1, g0 + j, codes[:, j, :], 3, t, False, g0 + j == GROUPS - 1)
+            og = work.tile([P, NT], F32, name="gate", tag="gate")
+            add_bias(og, accs[t], 3, t)
+            nc.scalar.activation(out=og[:], in_=og[:], func=FUNC.Sigmoid)
+            ogs.append(og)
+
+        def o_back(t):
+            nc.vector.tensor_tensor(out=ogs[t][:], in0=ogs[t][:], in1=si[t][:], op=ALU.mult)
+            queue = nc.sync if t == TILES - 1 else nc.gpsimd
+            queue.dma_start(out=out_0[:, t * NT : (t + 1) * NT], in_=ogs[t][:])
+
+        for t in range(TILES):
+            o_front(t)
+            if t > 0:
+                o_back(t - 1)
+        o_back(TILES - 1)

@@ -30,6 +30,14 @@ def load_scale_row_set(nc, plane, scales, r):
     )
 
 
+def load_scale_row_pair(nc, plane, scales, row, g0, ng):
+    p0 = 32 * (row // 4) + row % 4
+    nc.sync.dma_start(
+        out=plane[p0:P:64, g0 : g0 + ng, :].bitcast(I32),
+        in_=scales[g0 : g0 + ng, row:16:8, :].rearrange("g q n -> q g n").bitcast(I32),
+    )
+
+
 def load_codes(nc, pool, words, g0, ng, c0, nbytes):
     codes = pool.tile([P, ng, nbytes], U8, name="codes", tag="codes", align_bytes=64)
     nc.sync.dma_start(
@@ -114,10 +122,18 @@ def tile_multilayerlstmcell_pa_kernel(
 
         def load_pair_scales(pair):
             for m in range(2):
-                for r in range(4):
-                    load_scale_row_set(
-                        nc, planes[m][pair], w_scales[m][:, :, pair * PAIR : (pair + 1) * PAIR], r
-                    )
+                for row in range(8):
+                    pieces = 2 if m == 1 and row >= 4 else 1
+                    ng = GROUPS // pieces
+                    for piece in range(pieces):
+                        load_scale_row_pair(
+                            nc,
+                            planes[m][pair],
+                            w_scales[m][:, :, pair * PAIR : (pair + 1) * PAIR],
+                            row,
+                            piece * ng,
+                            ng,
+                        )
 
         def mx_pass(acc, m, g, codes_ap, gate, t, start, stop):
             col = (gate % 2) * H + t * NT
@@ -247,7 +263,7 @@ def tile_multilayerlstmcell_pa_kernel(
 
         def o_back(t):
             nc.vector.tensor_tensor(out=ogs[t][:], in0=ogs[t][:], in1=si[t][:], op=ALU.mult)
-            queue = nc.sync if t == TILES - 1 else nc.gpsimd
+            queue = (nc.gpsimd, nc.gpsimd, nc.scalar, nc.sync)[t]
             queue.dma_start(out=out_0[:, t * NT : (t + 1) * NT], in_=ogs[t][:])
 
         for t in range(TILES):

@@ -20,21 +20,13 @@ TILES = H // NT
 GROUPS = 4
 GATE_BYTES = 2 * H
 TILE_BYTES = 2 * NT
-PAIR = 2 * H
 
 
-def load_scale_row_set(nc, plane, scales, r):
-    nc.sync.dma_start(
-        out=plane[r:P:32, :, :].bitcast(I32),
-        in_=scales[:, r:16:4, :].rearrange("g q n -> q g n").bitcast(I32),
-    )
-
-
-def load_scale_row_pair(nc, plane, scales, row, g0, ng):
+def load_scale_rows(nc, plane, scales, row, row_step, g0, ng):
     p0 = 32 * (row // 4) + row % 4
     nc.sync.dma_start(
-        out=plane[p0:P:64, g0 : g0 + ng, :].bitcast(I32),
-        in_=scales[g0 : g0 + ng, row:16:8, :].rearrange("g q n -> q g n").bitcast(I32),
+        out=plane[p0 : P : 8 * row_step, g0 : g0 + ng, :].bitcast(I32),
+        in_=scales[g0 : g0 + ng, row:16:row_step, :].rearrange("g q n -> q g n").bitcast(I32),
     )
 
 
@@ -89,7 +81,7 @@ def tile_multilayerlstmcell_pa_kernel(
 
         a_codes = []
         a_plane = []
-        for m, (words, label) in enumerate(((lstm_input_words, "x"), (h_prev_words, "h"))):
+        for words, label in ((lstm_input_words, "x"), (h_prev_words, "h")):
             codes = const.tile([P, GROUPS, 2 * P], U8, name="acodes_" + label, align_bytes=64)
             plane = const.tile([P, GROUPS, P], U8, name="aplane_" + label, align_bytes=64)
             nc.vector.memset(plane[:].rearrange("p g n -> p (g n)").bitcast(I32), 0)
@@ -99,74 +91,50 @@ def tile_multilayerlstmcell_pa_kernel(
             a_codes.append(codes)
             a_plane.append(plane)
 
-        planes = [[None, None], [None, None]]
+        planes = []
         sel = const.tile([P, 16], BF16, name="sel")
-        for pair in range(2):
-            for m in range(2):
-                plane = const.tile(
-                    [P, GROUPS, PAIR], U8, name="plane_%d_%d" % (m, pair), align_bytes=64
+        for m in range(2):
+            plane = const.tile([P, GROUPS, 4 * H], U8, name="plane_%d" % m, align_bytes=64)
+            nc.vector.memset(plane[:].rearrange("p g n -> p (g n)").bitcast(I32), 0)
+            planes.append(plane)
+            if m == 0:
+                nc.vector.tensor_tensor(
+                    out=sel[:], in0=ident[:, 0:16], in1=ident[:, 16:32], op=ALU.add
                 )
-                nc.vector.memset(plane[:].rearrange("p g n -> p (g n)").bitcast(I32), 0)
-                planes[m][pair] = plane
-                if pair == 0 and m == 0:
-                    nc.vector.tensor_tensor(
-                        out=sel[:], in0=ident[:, 0:16], in1=ident[:, 16:32], op=ALU.add
-                    )
 
-        def load_gate_codes(gate):
-            return [
-                load_codes(nc, stream, w_words[m], 2 * half, 2, gate * GATE_BYTES, GATE_BYTES)
-                for m in range(2)
-                for half in range(2)
-            ]
-
-        def load_pair_scales(pair):
-            for m in range(2):
-                for row in range(8):
-                    pieces = 2 if m == 1 and row >= 4 else 1
-                    ng = GROUPS // pieces
-                    for piece in range(pieces):
-                        load_scale_row_pair(
-                            nc,
-                            planes[m][pair],
-                            w_scales[m][:, :, pair * PAIR : (pair + 1) * PAIR],
-                            row,
-                            piece * ng,
-                            ng,
-                        )
-
-        def mx_pass(acc, m, g, codes_ap, gate, t, start, stop):
-            col = (gate % 2) * H + t * NT
+        def mx_pass(acc, m, g, codes_ap, gate, t):
+            col = gate * H + t * NT
             nc.tensor.matmul_mx(
                 out=acc[:],
                 lhsT=a_codes[m][:, g, :].bitcast(FP4X4),
                 lhsT_scale=a_plane[m][:, g, :],
                 rhs=codes_ap.bitcast(FP4X4),
-                rhs_scale=planes[m][gate // 2][:, g, col : col + NT],
-                start=start,
-                stop=stop,
+                rhs_scale=planes[m][:, g, col : col + NT],
+                start=(m == 0 and g == 0),
+                stop=(m == 1 and g == GROUPS - 1),
             )
 
         def new_accs():
             return [psum.tile([P, NT], F32, name="acc", tag="acc") for t in range(TILES)]
 
-        def gate_matmuls(gate, chunks, accs, ms):
-            for m in ms:
-                for half in range(2):
-                    chunk = chunks[2 * m + half]
-                    for j in range(2):
-                        g = 2 * half + j
-                        for t in range(TILES):
-                            mx_pass(
-                                accs[t],
-                                m,
-                                g,
-                                chunk[:, j, t * TILE_BYTES : (t + 1) * TILE_BYTES],
-                                gate,
-                                t,
-                                m == 0 and g == 0,
-                                m == 1 and g == GROUPS - 1,
-                            )
+        def load_half_gate(m, gate):
+            return [
+                load_codes(nc, stream, w_words[m], 2 * half, 2, gate * GATE_BYTES, GATE_BYTES)
+                for half in range(2)
+            ]
+
+        def half_gate_matmuls(m, gate, chunks, accs):
+            for half in range(2):
+                for j in range(2):
+                    for t in range(TILES):
+                        mx_pass(
+                            accs[t],
+                            m,
+                            2 * half + j,
+                            chunks[half][:, j, t * TILE_BYTES : (t + 1) * TILE_BYTES],
+                            gate,
+                            t,
+                        )
 
         def add_bias(dst, acc, gate, t):
             nc.vector.tensor_tensor(
@@ -174,12 +142,17 @@ def tile_multilayerlstmcell_pa_kernel(
             )
 
         small = [(a_plane[m], sc, r) for m, sc in enumerate((lstm_input_scales, h_prev_scales)) for r in range(4)]
-        chunks_i = []
-        for n in range(4):
-            chunks_i.append(load_codes(nc, stream, w_words[n // 2], 2 * (n % 2), 2, 0, GATE_BYTES))
-            for plane, sc, r in small[2 * n : 2 * n + 2]:
-                load_scale_row_set(nc, plane, sc, r)
-        load_pair_scales(0)
+        chunks_if = []
+        for g in range(GROUPS):
+            chunks_if.append(load_codes(nc, stream, w_ih_words, g, 1, 0, 2 * GATE_BYTES))
+            for plane, sc, r in small[2 * g : 2 * g + 2]:
+                load_scale_rows(nc, plane, sc, r, 4, 0, GROUPS)
+
+        for m in range(2):
+            for row in range(8):
+                ng = 1 if m == 1 and row >= 6 else GROUPS
+                for g0 in range(0, GROUPS, ng):
+                    load_scale_rows(nc, planes[m], w_scales[m], row, 8, g0, ng)
 
         bias = const.tile([P, 4 * TILES, NT], F32, name="bias")
         for c in range(4 * TILES):
@@ -193,24 +166,30 @@ def tile_multilayerlstmcell_pa_kernel(
             )
             nc.scalar.copy(out=bias[:, c, :], in_=bacc[:])
 
-        chunks_f = load_gate_codes(1)
+        chunks_i = load_half_gate(1, 0)
+        chunks_f = load_half_gate(1, 1)
 
-        accs = new_accs()
-        gate_matmuls(0, chunks_i, accs, (0, 1))
+        accs_i = new_accs()
+        accs_f = new_accs()
+        for g in range(GROUPS):
+            for gate, accs in ((0, accs_i), (1, accs_f)):
+                for t in range(TILES):
+                    c0 = gate * GATE_BYTES + t * TILE_BYTES
+                    mx_pass(accs[t], 0, g, chunks_if[g][:, 0, c0 : c0 + TILE_BYTES], gate, t)
+
+        half_gate_matmuls(1, 0, chunks_i, accs_i)
         si = [const.tile([P, NT], F32, name="si%d" % t) for t in range(TILES)]
         for t in range(TILES):
-            add_bias(si[t], accs[t], 0, t)
+            add_bias(si[t], accs_i[t], 0, t)
         for t in range(TILES):
             nc.scalar.activation(out=si[t][:], in_=si[t][:], func=FUNC.Sigmoid)
 
-        load_pair_scales(1)
-        chunks_g = load_gate_codes(2)
+        chunks_g = load_half_gate(0, 2) + load_half_gate(1, 2)
 
-        accs = new_accs()
-        gate_matmuls(1, chunks_f, accs, (0, 1))
+        half_gate_matmuls(1, 1, chunks_f, accs_f)
         fc = [const.tile([P, NT], F32, name="fc%d" % t) for t in range(TILES)]
         for t in range(TILES):
-            add_bias(fc[t], accs[t], 1, t)
+            add_bias(fc[t], accs_f[t], 1, t)
         for t in range(TILES):
             nc.scalar.activation(out=fc[t][:], in_=fc[t][:], func=FUNC.Sigmoid)
         for t in range(TILES):
@@ -219,14 +198,15 @@ def tile_multilayerlstmcell_pa_kernel(
             )
 
         o_col = 3 * GATE_BYTES
-        chunks_o = [load_codes(nc, stream, w_ih_words, 2 * half, 2, o_col, GATE_BYTES) for half in range(2)]
+        chunks_o = load_half_gate(0, 3)
         o_hh = [
             [(load_codes(nc, stream, w_hh_words, 0, GROUPS, o_col + t * TILE_BYTES, TILE_BYTES), 0, GROUPS)]
             for t in range(2)
         ]
 
         accs = new_accs()
-        gate_matmuls(2, chunks_g, accs, (0, 1))
+        half_gate_matmuls(0, 2, chunks_g[0:2], accs)
+        half_gate_matmuls(1, 2, chunks_g[2:4], accs)
         cand = [work.tile([P, NT], F32, name="gate", tag="gate") for t in range(TILES)]
         for t in range(TILES):
             add_bias(cand[t], accs[t], 2, t)
@@ -235,7 +215,6 @@ def tile_multilayerlstmcell_pa_kernel(
         for t in range(TILES):
             nc.vector.tensor_tensor(out=cand[t][:], in0=cand[t][:], in1=si[t][:], op=ALU.mult)
             nc.vector.tensor_tensor(out=fc[t][:], in0=cand[t][:], in1=fc[t][:], op=ALU.add)
-            nc.gpsimd.dma_start(out=out_1[:, t * NT : (t + 1) * NT], in_=fc[t][:])
             nc.scalar.activation(out=si[t][:], in_=fc[t][:], func=FUNC.Tanh)
 
         o_hh.append(
@@ -248,14 +227,17 @@ def tile_multilayerlstmcell_pa_kernel(
             ]
         )
 
+        for t in range(TILES):
+            nc.sync.dma_start(out=out_1[:, t * NT : (t + 1) * NT], in_=fc[t][:])
+
         accs = new_accs()
-        gate_matmuls(3, chunks_o, accs, (0,))
+        half_gate_matmuls(0, 3, chunks_o, accs)
         ogs = []
 
         def o_front(t):
             for codes, g0, ng in o_hh[t]:
                 for j in range(ng):
-                    mx_pass(accs[t], 1, g0 + j, codes[:, j, :], 3, t, False, g0 + j == GROUPS - 1)
+                    mx_pass(accs[t], 1, g0 + j, codes[:, j, :], 3, t)
             og = work.tile([P, NT], F32, name="gate", tag="gate")
             add_bias(og, accs[t], 3, t)
             nc.scalar.activation(out=og[:], in_=og[:], func=FUNC.Sigmoid)

@@ -166,18 +166,17 @@ def tile_multilayerlstmcell_pa_kernel(
             )
             nc.scalar.copy(out=bias[:, c, :], in_=bacc[:])
 
-        chunks_i = load_half_gate(1, 0)
-        chunks_f = load_half_gate(1, 1)
+        chunks_if_hh = [load_codes(nc, stream, w_hh_words, g, 1, 0, 2 * GATE_BYTES) for g in range(GROUPS)]
 
         accs_i = new_accs()
         accs_f = new_accs()
-        for g in range(GROUPS):
-            for gate, accs in ((0, accs_i), (1, accs_f)):
-                for t in range(TILES):
-                    c0 = gate * GATE_BYTES + t * TILE_BYTES
-                    mx_pass(accs[t], 0, g, chunks_if[g][:, 0, c0 : c0 + TILE_BYTES], gate, t)
+        for m, chunks in ((0, chunks_if), (1, chunks_if_hh)):
+            for g in range(GROUPS):
+                for gate, accs in ((0, accs_i), (1, accs_f)):
+                    for t in range(TILES):
+                        c0 = gate * GATE_BYTES + t * TILE_BYTES
+                        mx_pass(accs[t], m, g, chunks[g][:, 0, c0 : c0 + TILE_BYTES], gate, t)
 
-        half_gate_matmuls(1, 0, chunks_i, accs_i)
         si = [const.tile([P, NT], F32, name="si%d" % t) for t in range(TILES)]
         for t in range(TILES):
             add_bias(si[t], accs_i[t], 0, t)
@@ -186,8 +185,8 @@ def tile_multilayerlstmcell_pa_kernel(
 
         chunks_g = load_half_gate(0, 2) + load_half_gate(1, 2)
 
-        half_gate_matmuls(1, 1, chunks_f, accs_f)
-        fc = [const.tile([P, NT], F32, name="fc%d" % t) for t in range(TILES)]
+        fc_all = const.tile([P, TILES, NT], F32, name="fc_all")
+        fc = [fc_all[:, t, :] for t in range(TILES)]
         for t in range(TILES):
             add_bias(fc[t], accs_f[t], 1, t)
         for t in range(TILES):
@@ -227,8 +226,7 @@ def tile_multilayerlstmcell_pa_kernel(
             ]
         )
 
-        for t in range(TILES):
-            nc.sync.dma_start(out=out_1[:, t * NT : (t + 1) * NT], in_=fc[t][:])
+        nc.sync.dma_start(out=out_1, in_=fc_all[:].rearrange("p t n -> p (t n)"))
 
         accs = new_accs()
         half_gate_matmuls(0, 3, chunks_o, accs)

@@ -243,8 +243,7 @@ def tile_multilayerlstmcell_pa_kernel(
 
         def o_back(t):
             nc.vector.tensor_tensor(out=ogs[t][:], in0=ogs[t][:], in1=si[t][:], op=ALU.mult)
-            queue = (nc.gpsimd, nc.gpsimd, nc.scalar, nc.sync)[t]
-            queue.dma_start(out=out_0[:, t * NT : (t + 1) * NT], in_=ogs[t][:])
+            nc.sync.dma_start(out=out_0[:, t * NT : (t + 1) * NT], in_=ogs[t][:])
 
         for t in range(TILES):
             o_front(t)

@@ -183,7 +183,11 @@ def tile_multilayerlstmcell_pa_kernel(
         for t in range(TILES):
             nc.scalar.activation(out=si[t][:], in_=si[t][:], func=FUNC.Sigmoid)
 
-        chunks_g = load_half_gate(0, 2) + load_half_gate(1, 2)
+        chunks_g = load_half_gate(0, 2)
+        pairs_g = [
+            load_codes(nc, stream, w_hh_words, 0, GROUPS, 2 * GATE_BYTES + pair * 2 * TILE_BYTES, 2 * TILE_BYTES)
+            for pair in range(2)
+        ]
 
         fc_all = const.tile([P, TILES, NT], F32, name="fc_all")
         fc = [fc_all[:, t, :] for t in range(TILES)]
@@ -204,17 +208,22 @@ def tile_multilayerlstmcell_pa_kernel(
         ]
 
         accs = new_accs()
-        half_gate_matmuls(0, 2, chunks_g[0:2], accs)
-        half_gate_matmuls(1, 2, chunks_g[2:4], accs)
+        half_gate_matmuls(0, 2, chunks_g, accs)
         cand = [work.tile([P, NT], F32, name="gate", tag="gate") for t in range(TILES)]
-        for t in range(TILES):
-            add_bias(cand[t], accs[t], 2, t)
-        for t in range(TILES):
-            nc.scalar.activation(out=cand[t][:], in_=cand[t][:], func=FUNC.Tanh)
-        for t in range(TILES):
-            nc.vector.tensor_tensor(out=cand[t][:], in0=cand[t][:], in1=si[t][:], op=ALU.mult)
-            nc.vector.tensor_tensor(out=fc[t][:], in0=cand[t][:], in1=fc[t][:], op=ALU.add)
-            nc.scalar.activation(out=si[t][:], in_=fc[t][:], func=FUNC.Tanh)
+        for pair in range(2):
+            tiles = (2 * pair, 2 * pair + 1)
+            for g in range(GROUPS):
+                for t in tiles:
+                    c0 = (t % 2) * TILE_BYTES
+                    mx_pass(accs[t], 1, g, pairs_g[pair][:, g, c0 : c0 + TILE_BYTES], 2, t)
+            for t in tiles:
+                add_bias(cand[t], accs[t], 2, t)
+            for t in tiles:
+                nc.scalar.activation(out=cand[t][:], in_=cand[t][:], func=FUNC.Tanh)
+            for t in tiles:
+                nc.vector.tensor_tensor(out=cand[t][:], in0=cand[t][:], in1=si[t][:], op=ALU.mult)
+                nc.vector.tensor_tensor(out=fc[t][:], in0=cand[t][:], in1=fc[t][:], op=ALU.add)
+                nc.scalar.activation(out=si[t][:], in_=fc[t][:], func=FUNC.Tanh)
 
         o_hh.append(
             [(load_codes(nc, stream, w_hh_words, 0, GROUPS, o_col + 2 * TILE_BYTES, TILE_BYTES), 0, GROUPS)]

@@ -210,20 +210,23 @@ def tile_multilayerlstmcell_pa_kernel(
         accs = new_accs()
         half_gate_matmuls(0, 2, chunks_g, accs)
         cand = [work.tile([P, NT], F32, name="gate", tag="gate") for t in range(TILES)]
-        for pair in range(2):
-            tiles = (2 * pair, 2 * pair + 1)
+        def cand_front(t):
             for g in range(GROUPS):
-                for t in tiles:
-                    c0 = (t % 2) * TILE_BYTES
-                    mx_pass(accs[t], 1, g, pairs_g[pair][:, g, c0 : c0 + TILE_BYTES], 2, t)
-            for t in tiles:
-                add_bias(cand[t], accs[t], 2, t)
-            for t in tiles:
-                nc.scalar.activation(out=cand[t][:], in_=cand[t][:], func=FUNC.Tanh)
-            for t in tiles:
-                nc.vector.tensor_tensor(out=cand[t][:], in0=cand[t][:], in1=si[t][:], op=ALU.mult)
-                nc.vector.tensor_tensor(out=fc[t][:], in0=cand[t][:], in1=fc[t][:], op=ALU.add)
-                nc.scalar.activation(out=si[t][:], in_=fc[t][:], func=FUNC.Tanh)
+                c0 = (t % 2) * TILE_BYTES
+                mx_pass(accs[t], 1, g, pairs_g[t // 2][:, g, c0 : c0 + TILE_BYTES], 2, t)
+            add_bias(cand[t], accs[t], 2, t)
+            nc.scalar.activation(out=cand[t][:], in_=cand[t][:], func=FUNC.Tanh)
+
+        def cand_back(t):
+            nc.vector.tensor_tensor(out=cand[t][:], in0=cand[t][:], in1=si[t][:], op=ALU.mult)
+            nc.vector.tensor_tensor(out=fc[t][:], in0=cand[t][:], in1=fc[t][:], op=ALU.add)
+            nc.scalar.activation(out=si[t][:], in_=fc[t][:], func=FUNC.Tanh)
+
+        for t in range(TILES):
+            cand_front(t)
+            if t > 0:
+                cand_back(t - 1)
+        cand_back(TILES - 1)
 
         o_hh.append(
             [(load_codes(nc, stream, w_hh_words, 0, GROUPS, o_col + 2 * TILE_BYTES, TILE_BYTES), 0, GROUPS)]

@@ -240,25 +240,55 @@ def tile_multilayerlstmcell_pa_kernel(
 
         nc.sync.dma_start(out=out_1, in_=fc_all[:].rearrange("p t n -> p (t n)"))
 
-        accs = new_accs()
-        half_gate_matmuls(0, 3, chunks_o, accs)
-        ogs = []
+        last = TILES - 1
+        units = [(t * NT, NT) for t in range(last)] + [(last * NT + u * (NT // 2), NT // 2) for u in range(2)]
+        banks = [psum.tile([P, n], F32, name="acc", tag="acc") for c, n in units]
+        og_all = const.tile([P, H], F32, name="og_all")
+        bias_o = bias[:, 3 * TILES : 4 * TILES, :].rearrange("p t n -> p (t n)")
 
-        def o_front(t):
-            for codes, g0, ng in o_hh[t]:
-                for j in range(ng):
-                    mx_pass(accs[t], 1, g0 + j, codes[:, j, :], 3, t)
-            og = work.tile([P, NT], F32, name="gate", tag="gate")
-            add_bias(og, accs[t], 3, t)
-            nc.scalar.activation(out=og[:], in_=og[:], func=FUNC.Sigmoid)
-            ogs.append(og)
+        def o_pass(k, m, g, codes, j, c0):
+            c, n = units[k]
+            nc.tensor.matmul_mx(
+                out=banks[k][:],
+                lhsT=a_codes[m][:, g, :].bitcast(FP4X4),
+                lhsT_scale=a_plane[m][:, g, :],
+                rhs=codes[:, j, 2 * (c - c0) : 2 * (c - c0 + n)].bitcast(FP4X4),
+                rhs_scale=planes[m][:, g, 3 * H + c : 3 * H + c + n],
+                start=(m == 0 and g == 0),
+                stop=(m == 1 and g == GROUPS - 1),
+            )
 
-        def o_back(t):
-            nc.vector.tensor_tensor(out=ogs[t][:], in0=ogs[t][:], in1=si[t][:], op=ALU.mult)
-            nc.sync.dma_start(out=out_0[:, t * NT : (t + 1) * NT], in_=ogs[t][:])
+        def o_front(k):
+            c, n = units[k]
+            nc.vector.tensor_tensor(out=og_all[:, c : c + n], in0=banks[k][:], in1=bias_o[:, c : c + n], op=ALU.add)
+            nc.scalar.activation(out=og_all[:, c : c + n], in_=og_all[:, c : c + n], func=FUNC.Sigmoid)
 
-        for t in range(TILES):
-            o_front(t)
-            if t > 0:
-                o_back(t - 1)
-        o_back(TILES - 1)
+        def o_back(k):
+            c, n = units[k]
+            t = c // NT
+            nc.vector.tensor_tensor(
+                out=og_all[:, c : c + n], in0=og_all[:, c : c + n], in1=si[t][:, c - t * NT : c - t * NT + n], op=ALU.mult
+            )
+            nc.sync.dma_start(out=out_0[:, c : c + n], in_=og_all[:, c : c + n])
+
+        for half in range(2):
+            for j in range(2):
+                for k in range(len(units)):
+                    o_pass(k, 0, 2 * half + j, chunks_o[half], j, 0)
+        for k in range(last):
+            codes, g0, ng = o_hh[k][0]
+            for j in range(ng):
+                o_pass(k, 1, g0 + j, codes, j, k * NT)
+            o_front(k)
+            if k > 0:
+                o_back(k - 1)
+        early, late = o_hh[last]
+        for j in range(2):
+            for k in (last, last + 1):
+                o_pass(k, 1, j, early[0], j, last * NT)
+        for k in (last, last + 1):
+            for j in range(2):
+                o_pass(k, 1, 2 + j, late[0], j, last * NT)
+            o_front(k)
+        for k in (last - 1, last, last + 1):
+            o_back(k)

@@ -232,10 +232,7 @@ def tile_multilayerlstmcell_pa_kernel(
             [(load_codes(nc, stream, w_hh_words, 0, GROUPS, o_col + 2 * TILE_BYTES, TILE_BYTES), 0, GROUPS)]
         )
         o_hh.append(
-            [
-                (load_codes(nc, stream, w_hh_words, 2 * half, 2, o_col + 3 * TILE_BYTES, TILE_BYTES), 2 * half, 2)
-                for half in range(2)
-            ]
+            [(load_codes(nc, stream, w_hh_words, 0, GROUPS, o_col + 3 * TILE_BYTES, TILE_BYTES), 0, GROUPS)]
         )
 
         nc.sync.dma_start(out=out_1, in_=fc_all[:].rearrange("p t n -> p (t n)"))
@@ -282,13 +279,9 @@ def tile_multilayerlstmcell_pa_kernel(
             o_front(k)
             if k > 0:
                 o_back(k - 1)
-        early, late = o_hh[last]
-        for j in range(2):
-            for k in (last, last + 1):
-                o_pass(k, 1, j, early[0], j, last * NT)
         for k in (last, last + 1):
-            for j in range(2):
-                o_pass(k, 1, 2 + j, late[0], j, last * NT)
+            for j in range(GROUPS):
+                o_pass(k, 1, j, o_hh[last][0][0], j, last * NT)
             o_front(k)
         for k in (last - 1, last, last + 1):
             o_back(k)

@@ -62,7 +62,7 @@ def tile_multilayerlstmcell_pa_kernel(
     with ExitStack() as ctx:
         ctx.enter_context(tc.manual_schedule())
         const = ctx.enter_context(tc.tile_pool(name="const", bufs=1))
-        stream = ctx.enter_context(tc.tile_pool(name="stream", bufs=8))
+        stream = ctx.enter_context(tc.tile_pool(name="stream", bufs=12))
         work = ctx.enter_context(tc.tile_pool(name="work", bufs=4))
         psum = ctx.enter_context(tc.psum_pool(name="psum", bufs=8))
 

from contextlib import ExitStack

import concourse.masks as masks
import concourse.mybir as mybir

FLOPS = 2 * 128 * 4096 * 8192

F32 = mybir.dt.float32
BF16 = mybir.dt.bfloat16
U8 = mybir.dt.uint8
I32 = mybir.dt.int32
FP4X4 = mybir.dt.float4_e2m1fn_x4
FUNC = mybir.ActivationFunctionType
ALU = mybir.AluOpType

P = 128
H = 2048
NT = 512
TILES = H // NT
GROUPS = 4
GATE_BYTES = 2 * H
TILE_BYTES = 2 * NT


def load_scale_rows(nc, plane, scales, row, row_step, g0, ng):
    p0 = 32 * (row // 4) + row % 4
    nc.sync.dma_start(
        out=plane[p0 : P : 8 * row_step, g0 : g0 + ng, :].bitcast(I32),
        in_=scales[g0 : g0 + ng, row:16:row_step, :].rearrange("g q n -> q g n").bitcast(I32),
    )


def load_codes(nc, pool, words, g0, ng, c0, nbytes):
    codes = pool.tile([P, ng, nbytes], U8, name="codes", tag="codes", align_bytes=64)
    nc.sync.dma_start(
        out=codes[:].bitcast(I32),
        in_=words[g0 : g0 + ng, :, c0 : c0 + nbytes].rearrange("g p n -> p g n").bitcast(I32),
    )
    return codes


def tile_multilayerlstmcell_pa_kernel(
    tc,
    lstm_input_words,
    lstm_input_scales,
    h_prev_words,
    h_prev_scales,
    c_prev,
    w_ih_words,
    w_ih_scales,
    w_hh_words,
    w_hh_scales,
    b_ih,
    b_hh,
    out_0,
    out_1,
):
    nc = tc.nc
    w_words = (w_ih_words, w_hh_words)
    w_scales = (w_ih_scales, w_hh_scales)

    with ExitStack() as ctx:
        ctx.enter_context(tc.manual_schedule())
        const = ctx.enter_context(tc.tile_pool(name="const", bufs=1))
        stream = ctx.enter_context(tc.tile_pool(name="stream", bufs=12))
        work = ctx.enter_context(tc.tile_pool(name="work", bufs=4))
        psum = ctx.enter_context(tc.psum_pool(name="psum", bufs=8))

        brow = const.tile([P, NT], BF16, name="brow")
        nc.gpsimd.memset(brow[:], 0.0)
        ident = const.tile([P, P], BF16, name="ident")
        masks.make_identity(nc, ident[:])
        warm = const.tile([P, 1], F32, name="warm")
        nc.vector.memset(warm[:], 0.0)

        nc.scalar.dma_start(out=brow[0:16, :], in_=b_ih.rearrange("(c n) -> c n", c=16))
        nc.scalar.dma_start(out=brow[16:32, :], in_=b_hh.rearrange("(c n) -> c n", c=16))
        cprev = const.tile([P, H], BF16, name="cprev")
        nc.scalar.dma_start(out=cprev[:], in_=c_prev)
        nc.scalar.activation(out=warm[:], in_=warm[:], func=FUNC.Sigmoid)

        a_codes = []
        a_plane = []
        for words, label in ((lstm_input_words, "x"), (h_prev_words, "h")):
            codes = const.tile([P, GROUPS, 2 * P], U8, name="acodes_" + label, align_bytes=64)
            plane = const.tile([P, GROUPS, P], U8, name="aplane_" + label, align_bytes=64)
            nc.vector.memset(plane[:].rearrange("p g n -> p (g n)").bitcast(I32), 0)
            nc.sync.dma_start(
                out=codes[:].bitcast(I32), in_=words.rearrange("g p n -> p g n").bitcast(I32)
            )
            a_codes.append(codes)
            a_plane.append(plane)

        planes = []
        sel = const.tile([P, 16], BF16, name="sel")
        for m in range(2):
            plane = const.tile([P, GROUPS, 4 * H], U8, name="plane_%d" % m, align_bytes=64)
            nc.vector.memset(plane[:].rearrange("p g n -> p (g n)").bitcast(I32), 0)
            planes.append(plane)
            if m == 0:
                nc.vector.tensor_tensor(
                    out=sel[:], in0=ident[:, 0:16], in1=ident[:, 16:32], op=ALU.add
                )

        def mx_pass(acc, m, g, codes_ap, gate, t):
            col = gate * H + t * NT
            nc.tensor.matmul_mx(
                out=acc[:],
                lhsT=a_codes[m][:, g, :].bitcast(FP4X4),
                lhsT_scale=a_plane[m][:, g, :],
                rhs=codes_ap.bitcast(FP4X4),
                rhs_scale=planes[m][:, g, col : col + NT],
                start=(m == 0 and g == 0),
                stop=(m == 1 and g == GROUPS - 1),
            )

        def new_accs():
            return [psum.tile([P, NT], F32, name="acc", tag="acc") for t in range(TILES)]

        def load_half_gate(m, gate):
            return [
                load_codes(nc, stream, w_words[m], 2 * half, 2, gate * GATE_BYTES, GATE_BYTES)
                for half in range(2)
            ]

        def half_gate_matmuls(m, gate, chunks, accs):
            for half in range(2):
                for j in range(2):
                    for t in range(TILES):
                        mx_pass(
                            accs[t],
                            m,
                            2 * half + j,
                            chunks[half][:, j, t * TILE_BYTES : (t + 1) * TILE_BYTES],
                            gate,
                            t,
                        )

        def add_bias(dst, acc, gate, t):
            nc.vector.tensor_tensor(
                out=dst[:], in0=acc[:], in1=bias[:, gate * TILES + t, :], op=ALU.add
            )

        small = [(a_plane[m], sc, r) for m, sc in enumerate((lstm_input_scales, h_prev_scales)) for r in range(4)]
        chunks_if = []
        for g in range(GROUPS):
            chunks_if.append(load_codes(nc, stream, w_ih_words, g, 1, 0, 2 * GATE_BYTES))
            for plane, sc, r in small[2 * g : 2 * g + 2]:
                load_scale_rows(nc, plane, sc, r, 4, 0, GROUPS)

        for m in range(2):
            for row in range(8):
                ng = 1 if m == 1 and row >= 6 else GROUPS
                for g0 in range(0, GROUPS, ng):
                    load_scale_rows(nc, planes[m], w_scales[m], row, 8, g0, ng)

        bias = const.tile([P, 4 * TILES, NT], F32, name="bias")
        for c in range(4 * TILES):
            bacc = psum.tile([P, NT], F32, name="acc", tag="acc")
            nc.tensor.matmul(
                out=bacc[:],
                lhsT=sel[:, c : c + 1].to_broadcast([P, P]),
                rhs=brow[:],
                start=True,
                stop=True,
            )
            nc.scalar.copy(out=bias[:, c, :], in_=bacc[:])

        chunks_if_hh = [load_codes(nc, stream, w_hh_words, g, 1, 0, 2 * GATE_BYTES) for g in range(GROUPS)]

        accs_i = new_accs()
        accs_f = new_accs()
        for m, chunks in ((0, chunks_if), (1, chunks_if_hh)):
            for g in range(GROUPS):
                for gate, accs in ((0, accs_i), (1, accs_f)):
                    for t in range(TILES):
                        c0 = gate * GATE_BYTES + t * TILE_BYTES
                        mx_pass(accs[t], m, g, chunks[g][:, 0, c0 : c0 + TILE_BYTES], gate, t)

        si = [const.tile([P, NT], F32, name="si%d" % t) for t in range(TILES)]
        for t in range(TILES):
            add_bias(si[t], accs_i[t], 0, t)
        for t in range(TILES):
            nc.scalar.activation(out=si[t][:], in_=si[t][:], func=FUNC.Sigmoid)

        chunks_g = load_half_gate(0, 2)
        pairs_g = [
            load_codes(nc, stream, w_hh_words, 0, GROUPS, 2 * GATE_BYTES + pair * 2 * TILE_BYTES, 2 * TILE_BYTES)
            for pair in range(2)
        ]

        fc_all = const.tile([P, TILES, NT], F32, name="fc_all")
        fc = [fc_all[:, t, :] for t in range(TILES)]
        for t in range(TILES):
            add_bias(fc[t], accs_f[t], 1, t)
        for t in range(TILES):
            nc.scalar.activation(out=fc[t][:], in_=fc[t][:], func=FUNC.Sigmoid)
        for t in range(TILES):
            nc.vector.tensor_tensor(
                out=fc[t][:], in0=fc[t][:], in1=cprev[:, t * NT : (t + 1) * NT], op=ALU.mult
            )

        o_col = 3 * GATE_BYTES
        chunks_o = load_half_gate(0, 3)
        o_hh = [
            [(load_codes(nc, stream, w_hh_words, 0, GROUPS, o_col + t * TILE_BYTES, TILE_BYTES), 0, GROUPS)]
            for t in range(2)
        ]

        accs = new_accs()
        half_gate_matmuls(0, 2, chunks_g, accs)
        cand = [work.tile([P, NT], F32, name="gate", tag="gate") for t in range(TILES)]
        def cand_front(t):
            for g in range(GROUPS):
                c0 = (t % 2) * TILE_BYTES
                mx_pass(accs[t], 1, g, pairs_g[t // 2][:, g, c0 : c0 + TILE_BYTES], 2, t)
            add_bias(cand[t], accs[t], 2, t)
            nc.scalar.activation(out=cand[t][:], in_=cand[t][:], func=FUNC.Tanh)

        def cand_back(t):
            nc.vector.tensor_tensor(out=cand[t][:], in0=cand[t][:], in1=si[t][:], op=ALU.mult)
            nc.vector.tensor_tensor(out=fc[t][:], in0=cand[t][:], in1=fc[t][:], op=ALU.add)
            nc.scalar.activation(out=si[t][:], in_=fc[t][:], func=FUNC.Tanh)

        for t in range(TILES):
            cand_front(t)
            if t > 0:
                cand_back(t - 1)
        cand_back(TILES - 1)

        o_hh.append(
            [(load_codes(nc, stream, w_hh_words, 0, GROUPS, o_col + 2 * TILE_BYTES, TILE_BYTES), 0, GROUPS)]
        )
        o_hh.append(
            [(load_codes(nc, stream, w_hh_words, 0, GROUPS, o_col + 3 * TILE_BYTES, TILE_BYTES), 0, GROUPS)]
        )

        nc.sync.dma_start(out=out_1, in_=fc_all[:].rearrange("p t n -> p (t n)"))

        last = TILES - 1
        units = [(t * NT, NT) for t in range(last)] + [(last * NT + u * (NT // 2), NT // 2) for u in range(2)]
        banks = [psum.tile([P, n], F32, name="acc", tag="acc") for c, n in units]
        og_all = const.tile([P, H], F32, name="og_all")
        bias_o = bias[:, 3 * TILES : 4 * TILES, :].rearrange("p t n -> p (t n)")

        def o_pass(k, m, g, codes, j, c0):
            c, n = units[k]
            nc.tensor.matmul_mx(
                out=banks[k][:],
                lhsT=a_codes[m][:, g, :].bitcast(FP4X4),
                lhsT_scale=a_plane[m][:, g, :],
                rhs=codes[:, j, 2 * (c - c0) : 2 * (c - c0 + n)].bitcast(FP4X4),
                rhs_scale=planes[m][:, g, 3 * H + c : 3 * H + c + n],
                start=(m == 0 and g == 0),
                stop=(m == 1 and g == GROUPS - 1),
            )

        def o_front(k):
            c, n = units[k]
            nc.vector.tensor_tensor(out=og_all[:, c : c + n], in0=banks[k][:], in1=bias_o[:, c : c + n], op=ALU.add)
            nc.scalar.activation(out=og_all[:, c : c + n], in_=og_all[:, c : c + n], func=FUNC.Sigmoid)

        def o_back(k):
            c, n = units[k]
            t = c // NT
            nc.vector.tensor_tensor(
                out=og_all[:, c : c + n], in0=og_all[:, c : c + n], in1=si[t][:, c - t * NT : c - t * NT + n], op=ALU.mult
            )
            nc.sync.dma_start(out=out_0[:, c : c + n], in_=og_all[:, c : c + n])

        for half in range(2):
            for j in range(2):
                for k in range(len(units)):
                    o_pass(k, 0, 2 * half + j, chunks_o[half], j, 0)
        for k in range(last):
            codes, g0, ng = o_hh[k][0]
            for j in range(ng):
                o_pass(k, 1, g0 + j, codes, j, k * NT)
            o_front(k)
            if k > 0:
                o_back(k - 1)
        for k in (last, last + 1):
            for j in range(GROUPS):
                o_pass(k, 1, j, o_hh[last][0][0], j, last * NT)
            o_front(k)
        for k in (last - 1, last, last + 1):
            o_back(k)
